import numpy as np
import ml_dtypes

BF16 = ml_dtypes.bfloat16


def bf(x):
    return np.asarray(x, np.float32).astype(BF16)


def f32(x):
    return np.asarray(x, np.float32)


def f64(x):
    return np.asarray(x).astype(np.float64)


def striped(idx):
    return np.tile(idx.reshape(-1, 16).T, (8, 1))


C, S, N, I, T, H = 512, 512, 512, 256, 2, 4
BOUND = 1.0 / np.sqrt(T)


def setup_inputs():
    return {"x": f32(np.random.standard_normal((C, S))), "w": f32(np.random.uniform(-BOUND, BOUND, (H, N))), "bias": f32(np.random.uniform(-BOUND, BOUND, (H, I))), "offs": striped(np.random.permutation(np.tile(np.arange(S), 2))[:N])}


def reference(x, w, bias, offs):
    idx = offs[:16].T.reshape(-1)
    p = f64(x)[:, idx][:, None, :] * f64(w)[None, :, :]
    h = p[:, :, :I] + p[:, :, I:] + f64(bias)[None, :, :]
    return np.maximum(h, 0.0).reshape(C, H * I)

@@ -1,0 +1,53 @@
+import concourse.mybir as mybir
+
+F32 = mybir.dt.float32
+U16 = mybir.dt.uint16
+MULT = mybir.AluOpType.mult
+ADD = mybir.AluOpType.add
+RELU = mybir.ActivationFunctionType.Relu
+
+P = 128
+SAMPLES = 512
+FEATURES = 512
+ENTRIES = 512
+NETS = 256
+UNITS = 4
+BLOCKS = SAMPLES // P
+
+
+def tile_mlp_cutoff_kernel(tc, x, w, bias, offs, out):
+    nc = tc.nc
+    with (
+        tc.tile_pool(name="held", bufs=1) as held,
+        tc.tile_pool(name="work", bufs=2) as work,
+    ):
+        offsets = held.tile([P, ENTRIES // 16], U16, name="offsets")
+        nc.sync.dma_start(offsets[:], offs)
+
+        x_blocks = []
+        for b in range(BLOCKS):
+            x_block = held.tile([P, FEATURES], F32, name=f"x_block{b}")
+            nc.sync.dma_start(x_block[:], x[b * P : (b + 1) * P, :])
+            x_blocks.append(x_block)
+
+        w_rows = held.tile([P, UNITS, ENTRIES], F32, name="w_rows")
+        for o in range(UNITS):
+            nc.scalar.dma_start(w_rows[:, o, :], w[o, :].partition_broadcast(P))
+
+        bias_rows = held.tile([P, UNITS, NETS], F32, name="bias_rows")
+        for o in range(UNITS):
+            nc.scalar.dma_start(bias_rows[:, o, :], bias[o, :].partition_broadcast(P))
+
+        for b in range(BLOCKS):
+            products = work.tile([P, UNITS, ENTRIES], F32, name="products")
+            for o in range(UNITS):
+                nc.vector.tensor_tensor(
+                    products[:, o, :], x_blocks[b][:].indirect(offsets[:]), w_rows[:, o, :], MULT
+                )
+
+            hidden = work.tile([P, UNITS, NETS], F32, name="hidden")
+            nc.vector.tensor_tensor(hidden[:], products[:, :, 0:NETS], products[:, :, NETS:ENTRIES], ADD)
+            nc.vector.tensor_tensor(hidden[:], hidden[:], bias_rows[:], ADD)
+
+            nc.scalar.activation(hidden[:], hidden[:], RELU)
+            nc.sync.dma_start(out[b * P : (b + 1) * P, :], hidden[:].rearrange("p o i -> p (o i)"))

@@ -1,4 +1,5 @@
 import concourse.mybir as mybir
+from concourse.masks import make_identity
 
 F32 = mybir.dt.float32
 U16 = mybir.dt.uint16
@@ -14,12 +15,15 @@ NETS = 256
 UNITS = 4
 BLOCKS = SAMPLES // P
 
+TENSOR_UNITS = 3
+
 
 def tile_mlp_cutoff_kernel(tc, x, w, bias, offs, out):
     nc = tc.nc
     with (
         tc.tile_pool(name="held", bufs=1) as held,
-        tc.tile_pool(name="work", bufs=2) as work,
+        tc.tile_pool(name="work", bufs=4) as work,
+        tc.psum_pool(name="psum", bufs=4) as psum,
     ):
         offsets = held.tile([P, ENTRIES // 16], U16, name="offsets")
         nc.sync.dma_start(offsets[:], offs)
@@ -38,16 +42,25 @@ def tile_mlp_cutoff_kernel(tc, x, w, bias, offs, out):
         for o in range(UNITS):
             nc.scalar.dma_start(bias_rows[:, o, :], bias[o, :].partition_broadcast(P))
 
+        identity = held.tile([P, P], F32, name="identity")
+        make_identity(nc, identity[:])
+
         for b in range(BLOCKS):
-            products = work.tile([P, UNITS, ENTRIES], F32, name="products")
             for o in range(UNITS):
-                nc.vector.tensor_tensor(
-                    products[:, o, :], x_blocks[b][:].indirect(offsets[:]), w_rows[:, o, :], MULT
-                )
+                products = work.tile([P, ENTRIES], F32, name="products")
+                nc.vector.tensor_tensor(products[:], x_blocks[b][:].indirect(offsets[:]), w_rows[:, o, :], MULT)
+                first, second = products[:, 0:NETS], products[:, NETS:ENTRIES]
 
-            hidden = work.tile([P, UNITS, NETS], F32, name="hidden")
-            nc.vector.tensor_tensor(hidden[:], products[:, :, 0:NETS], products[:, :, NETS:ENTRIES], ADD)
-            nc.vector.tensor_tensor(hidden[:], hidden[:], bias_rows[:], ADD)
+                hidden = work.tile([P, NETS], F32, name="hidden")
+                if o < TENSOR_UNITS:
+                    total = psum.tile([P, NETS], F32, name="total")
+                    nc.tensor.matmul(total[:], identity[:], bias_rows[:, o, :], start=True, stop=False)
+                    nc.tensor.matmul(total[:], identity[:], first, start=False, stop=False)
+                    nc.tensor.matmul(total[:], identity[:], second, start=False, stop=True)
+                    nc.scalar.activation(hidden[:], total[:], RELU)
+                else:
+                    nc.vector.tensor_tensor(hidden[:], first, second, ADD)
+                    nc.vector.tensor_tensor(hidden[:], hidden[:], bias_rows[:, o, :], ADD)
+                    nc.scalar.activation(hidden[:], hidden[:], RELU)
 
-            nc.scalar.activation(hidden[:], hidden[:], RELU)
-            nc.sync.dma_start(out[b * P : (b + 1) * P, :], hidden[:].rearrange("p o i -> p (o i)"))
+                nc.sync.dma_start(out[b * P : (b + 1) * P, o * NETS : (o + 1) * NETS], hidden[:])

@@ -22,25 +22,23 @@ def tile_mlp_cutoff_kernel(tc, x, w, bias, offs, out):
     nc = tc.nc
     with (
         tc.tile_pool(name="held", bufs=1) as held,
-        tc.tile_pool(name="work", bufs=4) as work,
-        tc.psum_pool(name="psum", bufs=4) as psum,
+        tc.tile_pool(name="work", bufs=12) as work,
+        tc.psum_pool(name="psum", bufs=8) as psum,
     ):
         offsets = held.tile([P, ENTRIES // 16], U16, name="offsets")
         nc.sync.dma_start(offsets[:], offs)
 
-        x_blocks = []
-        for b in range(BLOCKS):
-            x_block = held.tile([P, FEATURES], F32, name=f"x_block{b}")
-            nc.sync.dma_start(x_block[:], x[b * P : (b + 1) * P, :])
-            x_blocks.append(x_block)
-
+        x_blocks = [held.tile([P, FEATURES], F32, name=f"x_block{b}") for b in range(BLOCKS)]
         w_rows = held.tile([P, UNITS, ENTRIES], F32, name="w_rows")
-        for o in range(UNITS):
-            nc.scalar.dma_start(w_rows[:, o, :], w[o, :].partition_broadcast(P))
+        bias_rows = held.tile([P, UNITS * NETS], F32, name="bias_rows")
 
-        bias_rows = held.tile([P, UNITS, NETS], F32, name="bias_rows")
-        for o in range(UNITS):
-            nc.scalar.dma_start(bias_rows[:, o, :], bias[o, :].partition_broadcast(P))
+        x_loads = [(x_blocks[b][:], x[b * P : (b + 1) * P, :]) for b in range(BLOCKS)]
+        w_loads = [(w_rows[:, o, :], w[o, :].partition_broadcast(P)) for o in range(UNITS)]
+        bias_load = (bias_rows[:], bias.rearrange("o i -> (o i)").partition_broadcast(P))
+        loads = [x_loads[0], w_loads[0], w_loads[1], bias_load] + w_loads[2:] + x_loads[1:]
+        for k, (tile_ap, source) in enumerate(loads):
+            queue = nc.sync if k % 2 == 0 else nc.scalar
+            queue.dma_start(tile_ap, source)
 
         identity = held.tile([P, P], F32, name="identity")
         make_identity(nc, identity[:])
@@ -50,17 +48,18 @@ def tile_mlp_cutoff_kernel(tc, x, w, bias, offs, out):
                 products = work.tile([P, ENTRIES], F32, name="products")
                 nc.vector.tensor_tensor(products[:], x_blocks[b][:].indirect(offsets[:]), w_rows[:, o, :], MULT)
                 first, second = products[:, 0:NETS], products[:, NETS:ENTRIES]
+                unit_bias = bias_rows[:, o * NETS : (o + 1) * NETS]
 
                 hidden = work.tile([P, NETS], F32, name="hidden")
                 if o < TENSOR_UNITS:
                     total = psum.tile([P, NETS], F32, name="total")
-                    nc.tensor.matmul(total[:], identity[:], bias_rows[:, o, :], start=True, stop=False)
-                    nc.tensor.matmul(total[:], identity[:], first, start=False, stop=False)
-                    nc.tensor.matmul(total[:], identity[:], second, start=False, stop=True)
+                    nc.tensor.matmul(total[:], identity[:], first, start=True, stop=False)
+                    nc.tensor.matmul(total[:], identity[:], second, start=False, stop=False)
+                    nc.tensor.matmul(total[:], identity[:], unit_bias, start=False, stop=True)
                     nc.scalar.activation(hidden[:], total[:], RELU)
                 else:
                     nc.vector.tensor_tensor(hidden[:], first, second, ADD)
-                    nc.vector.tensor_tensor(hidden[:], hidden[:], bias_rows[:, o, :], ADD)
+                    nc.vector.tensor_tensor(hidden[:], hidden[:], unit_bias, ADD)
                     nc.scalar.activation(hidden[:], hidden[:], RELU)
 
                 nc.sync.dma_start(out[b * P : (b + 1) * P, o * NETS : (o + 1) * NETS], hidden[:])

@@ -4,7 +4,6 @@ from concourse.masks import make_identity
 F32 = mybir.dt.float32
 U16 = mybir.dt.uint16
 MULT = mybir.AluOpType.mult
-ADD = mybir.AluOpType.add
 RELU = mybir.ActivationFunctionType.Relu
 
 P = 128
@@ -14,52 +13,71 @@ ENTRIES = 512
 NETS = 256
 UNITS = 4
 BLOCKS = SAMPLES // P
-
-TENSOR_UNITS = 3
+CHUNKS = NETS // P
 
 
 def tile_mlp_cutoff_kernel(tc, x, w, bias, offs, out):
     nc = tc.nc
     with (
         tc.tile_pool(name="held", bufs=1) as held,
-        tc.tile_pool(name="work", bufs=12) as work,
-        tc.psum_pool(name="psum", bufs=8) as psum,
+        tc.tile_pool(name="work", bufs=4) as work,
+        tc.psum_pool(name="psum", bufs=4) as psum,
     ):
         offsets = held.tile([P, ENTRIES // 16], U16, name="offsets")
         nc.sync.dma_start(offsets[:], offs)
 
         x_blocks = [held.tile([P, FEATURES], F32, name=f"x_block{b}") for b in range(BLOCKS)]
         w_rows = held.tile([P, UNITS, ENTRIES], F32, name="w_rows")
-        bias_rows = held.tile([P, UNITS * NETS], F32, name="bias_rows")
-
-        x_loads = [(x_blocks[b][:], x[b * P : (b + 1) * P, :]) for b in range(BLOCKS)]
-        w_loads = [(w_rows[:, o, :], w[o, :].partition_broadcast(P)) for o in range(UNITS)]
-        bias_load = (bias_rows[:], bias.rearrange("o i -> (o i)").partition_broadcast(P))
-        loads = [x_loads[0], w_loads[0], w_loads[1], bias_load] + w_loads[2:] + x_loads[1:]
-        for k, (tile_ap, source) in enumerate(loads):
-            queue = nc.sync if k % 2 == 0 else nc.scalar
-            queue.dma_start(tile_ap, source)
+        bias_columns = held.tile([P, UNITS * CHUNKS], F32, name="bias_columns")
+        nc.sync.dma_start(x_blocks[0][:], x[0:P, :])
+        nc.scalar.dma_start(w_rows[:, 0, :], w[0, :].partition_broadcast(P))
+        for b in range(1, BLOCKS):
+            nc.sync.dma_start(x_blocks[b][:], x[b * P : (b + 1) * P, :])
+        with nc.allow_non_contiguous_dma(reason="1,024 bias values, one to a partition"):
+            nc.scalar.dma_start(bias_columns[:], bias.rearrange("o (h p) -> p (o h)", p=P))
+        for o in range(1, UNITS):
+            nc.scalar.dma_start(w_rows[:, o, :], w[o, :].partition_broadcast(P))
 
         identity = held.tile([P, P], F32, name="identity")
         make_identity(nc, identity[:])
 
-        for b in range(BLOCKS):
-            for o in range(UNITS):
-                products = work.tile([P, ENTRIES], F32, name="products")
-                nc.vector.tensor_tensor(products[:], x_blocks[b][:].indirect(offsets[:]), w_rows[:, o, :], MULT)
-                first, second = products[:, 0:NETS], products[:, NETS:ENTRIES]
-                unit_bias = bias_rows[:, o * NETS : (o + 1) * NETS]
+        def products_summed(o, b):
+            products = work.tile([P, ENTRIES], F32, name="products")
+            nc.vector.tensor_tensor(products[:], x_blocks[b][:].indirect(offsets[:]), w_rows[:, o, :], MULT)
+            total_t = psum.tile([P, CHUNKS, P], F32, name="total_t")
+            for h in range(CHUNKS):
+                first = products[:, h * P : (h + 1) * P]
+                second = products[:, NETS + h * P : NETS + (h + 1) * P]
+                nc.tensor.matmul(total_t[:, h, :], first, identity[:], is_transpose=True, start=True, stop=False)
+                nc.tensor.matmul(total_t[:, h, :], second, identity[:], is_transpose=True, start=False, stop=True)
+            return total_t
 
-                hidden = work.tile([P, NETS], F32, name="hidden")
-                if o < TENSOR_UNITS:
-                    total = psum.tile([P, NETS], F32, name="total")
-                    nc.tensor.matmul(total[:], identity[:], first, start=True, stop=False)
-                    nc.tensor.matmul(total[:], identity[:], second, start=False, stop=False)
-                    nc.tensor.matmul(total[:], identity[:], unit_bias, start=False, stop=True)
-                    nc.scalar.activation(hidden[:], total[:], RELU)
-                else:
-                    nc.vector.tensor_tensor(hidden[:], first, second, ADD)
-                    nc.vector.tensor_tensor(hidden[:], hidden[:], unit_bias, ADD)
-                    nc.scalar.activation(hidden[:], hidden[:], RELU)
+        def bias_and_relu(o, total_t):
+            hidden_t = work.tile([P, CHUNKS, P], F32, name="hidden_t")
+            for h in range(CHUNKS):
+                column = o * CHUNKS + h
+                nc.scalar.activation(hidden_t[:, h, :], total_t[:, h, :], RELU, bias=bias_columns[:, column : column + 1])
+            return hidden_t
 
-                nc.sync.dma_start(out[b * P : (b + 1) * P, o * NETS : (o + 1) * NETS], hidden[:])
+        def back(hidden_t):
+            hidden_psum = psum.tile([P, NETS], F32, name="hidden_psum")
+            for h in range(CHUNKS):
+                nc.tensor.transpose(hidden_psum[:, h * P : (h + 1) * P], hidden_t[:, h, :], identity[:])
+            return hidden_psum
+
+        def copy_and_store(o, b, hidden_psum):
+            hidden = work.tile([P, NETS], F32, name="hidden")
+            nc.scalar.copy(hidden[:], hidden_psum[:])
+            nc.sync.dma_start(out[b * P : (b + 1) * P, o * NETS : (o + 1) * NETS], hidden[:])
+
+        earlier = None
+        for o in range(UNITS):
+            for b in range(BLOCKS):
+                total_t = products_summed(o, b)
+                if earlier is not None:
+                    hidden_psum = back(earlier[2])
+                hidden_t = bias_and_relu(o, total_t)
+                if earlier is not None:
+                    copy_and_store(earlier[0], earlier[1], hidden_psum)
+                earlier = (o, b, hidden_t)
+        copy_and_store(earlier[0], earlier[1], back(earlier[2]))

@@ -70,14 +70,9 @@ def tile_mlp_cutoff_kernel(tc, x, w, bias, offs, out):
             nc.scalar.copy(hidden[:], hidden_psum[:])
             nc.sync.dma_start(out[b * P : (b + 1) * P, o * NETS : (o + 1) * NETS], hidden[:])
 
-        earlier = None
         for o in range(UNITS):
             for b in range(BLOCKS):
                 total_t = products_summed(o, b)
-                if earlier is not None:
-                    hidden_psum = back(earlier[2])
                 hidden_t = bias_and_relu(o, total_t)
-                if earlier is not None:
-                    copy_and_store(earlier[0], earlier[1], hidden_psum)
-                earlier = (o, b, hidden_t)
-        copy_and_store(earlier[0], earlier[1], back(earlier[2]))
+                hidden_psum = back(hidden_t)
+                copy_and_store(o, b, hidden_psum)

@@ -4,6 +4,7 @@ from concourse.masks import make_identity
 F32 = mybir.dt.float32
 U16 = mybir.dt.uint16
 MULT = mybir.AluOpType.mult
+ADD = mybir.AluOpType.add
 RELU = mybir.ActivationFunctionType.Relu
 
 P = 128
@@ -38,12 +39,18 @@ def tile_mlp_cutoff_kernel(tc, x, w, bias, offs, out):
         for o in range(1, UNITS):
             nc.scalar.dma_start(w_rows[:, o, :], w[o, :].partition_broadcast(P))
 
+        last_bias_row = held.tile([P, NETS], F32, name="last_bias_row")
+        nc.scalar.dma_start(last_bias_row[:], bias[UNITS - 1, :].partition_broadcast(P))
+
         identity = held.tile([P, P], F32, name="identity")
         make_identity(nc, identity[:])
 
-        def products_summed(o, b):
+        def look_up(o, b):
             products = work.tile([P, ENTRIES], F32, name="products")
             nc.vector.tensor_tensor(products[:], x_blocks[b][:].indirect(offsets[:]), w_rows[:, o, :], MULT)
+            return products
+
+        def sum_transposed(products):
             total_t = psum.tile([P, CHUNKS, P], F32, name="total_t")
             for h in range(CHUNKS):
                 first = products[:, h * P : (h + 1) * P]
@@ -65,14 +72,23 @@ def tile_mlp_cutoff_kernel(tc, x, w, bias, offs, out):
                 nc.tensor.transpose(hidden_psum[:, h * P : (h + 1) * P], hidden_t[:, h, :], identity[:])
             return hidden_psum
 
-        def copy_and_store(o, b, hidden_psum):
+        def copy_out(hidden_psum):
             hidden = work.tile([P, NETS], F32, name="hidden")
             nc.scalar.copy(hidden[:], hidden_psum[:])
-            nc.sync.dma_start(out[b * P : (b + 1) * P, o * NETS : (o + 1) * NETS], hidden[:])
+            return hidden
+
+        def sum_bias_relu_on_vector(products):
+            hidden = work.tile([P, NETS], F32, name="hidden")
+            nc.vector.tensor_tensor(hidden[:], products[:, 0:NETS], products[:, NETS:ENTRIES], ADD)
+            nc.vector.tensor_tensor(hidden[:], hidden[:], last_bias_row[:], ADD)
+            nc.vector.tensor_scalar_max(hidden[:], hidden[:], 0.0)
+            return hidden
 
         for o in range(UNITS):
             for b in range(BLOCKS):
-                total_t = products_summed(o, b)
-                hidden_t = bias_and_relu(o, total_t)
-                hidden_psum = back(hidden_t)
-                copy_and_store(o, b, hidden_psum)
+                products = look_up(o, b)
+                if (o, b) == (UNITS - 1, BLOCKS - 1):
+                    hidden = sum_bias_relu_on_vector(products)
+                else:
+                    hidden = copy_out(back(bias_and_relu(o, sum_transposed(products))))
+                nc.sync.dma_start(out[b * P : (b + 1) * P, o * NETS : (o + 1) * NETS], hidden[:])

@@ -27,6 +27,7 @@ def tile_mlp_cutoff_kernel(tc, x, w, bias, offs, out):
         offsets = held.tile([P, ENTRIES // 16], U16, name="offsets")
         nc.sync.dma_start(offsets[:], offs)
 
+        pairs = sorted(((o, b) for o in range(UNITS) for b in range(BLOCKS)), key=max)
         x_blocks = [held.tile([P, FEATURES], F32, name=f"x_block{b}") for b in range(BLOCKS)]
         w_rows = held.tile([P, UNITS, ENTRIES], F32, name="w_rows")
         bias_columns = held.tile([P, UNITS * CHUNKS], F32, name="bias_columns")
@@ -84,11 +85,10 @@ def tile_mlp_cutoff_kernel(tc, x, w, bias, offs, out):
             nc.vector.tensor_scalar_max(hidden[:], hidden[:], 0.0)
             return hidden
 
-        for o in range(UNITS):
-            for b in range(BLOCKS):
-                products = look_up(o, b)
-                if (o, b) == (UNITS - 1, BLOCKS - 1):
-                    hidden = sum_bias_relu_on_vector(products)
-                else:
-                    hidden = copy_out(back(bias_and_relu(o, sum_transposed(products))))
-                nc.sync.dma_start(out[b * P : (b + 1) * P, o * NETS : (o + 1) * NETS], hidden[:])
+        for o, b in pairs:
+            products = look_up(o, b)
+            if (o, b) == pairs[-1]:
+                hidden = sum_bias_relu_on_vector(products)
+            else:
+                hidden = copy_out(back(bias_and_relu(o, sum_transposed(products))))
+            nc.sync.dma_start(out[b * P : (b + 1) * P, o * NETS : (o + 1) * NETS], hidden[:])

@@ -85,10 +85,19 @@ def tile_mlp_cutoff_kernel(tc, x, w, bias, offs, out):
             nc.vector.tensor_scalar_max(hidden[:], hidden[:], 0.0)
             return hidden
 
-        for o, b in pairs:
-            products = look_up(o, b)
-            if (o, b) == pairs[-1]:
-                hidden = sum_bias_relu_on_vector(products)
-            else:
-                hidden = copy_out(back(bias_and_relu(o, sum_transposed(products))))
+        def store(o, b, hidden):
             nc.sync.dma_start(out[b * P : (b + 1) * P, o * NETS : (o + 1) * NETS], hidden[:])
+
+        earlier = None
+        for o, b in pairs[:-1]:
+            total_t = sum_transposed(look_up(o, b))
+            if earlier is not None:
+                hidden_psum = back(earlier[2])
+            hidden_t = bias_and_relu(o, total_t)
+            if earlier is not None:
+                store(earlier[0], earlier[1], copy_out(hidden_psum))
+            earlier = (o, b, hidden_t)
+        o, b = pairs[-1]
+        products = look_up(o, b)
+        store(earlier[0], earlier[1], copy_out(back(earlier[2])))
+        store(o, b, sum_bias_relu_on_vector(products))

@@ -30,13 +30,13 @@ def tile_mlp_cutoff_kernel(tc, x, w, bias, offs, out):
         pairs = sorted(((o, b) for o in range(UNITS) for b in range(BLOCKS)), key=max)
         x_blocks = [held.tile([P, FEATURES], F32, name=f"x_block{b}") for b in range(BLOCKS)]
         w_rows = held.tile([P, UNITS, ENTRIES], F32, name="w_rows")
-        bias_columns = held.tile([P, UNITS * CHUNKS], F32, name="bias_columns")
+        bias_rows = held.tile([P, P], F32, name="bias_rows")
+        nc.vector.memset(bias_rows[:], 0.0)
         nc.sync.dma_start(x_blocks[0][:], x[0:P, :])
         nc.scalar.dma_start(w_rows[:, 0, :], w[0, :].partition_broadcast(P))
         for b in range(1, BLOCKS):
             nc.sync.dma_start(x_blocks[b][:], x[b * P : (b + 1) * P, :])
-        with nc.allow_non_contiguous_dma(reason="1,024 bias values, one to a partition"):
-            nc.scalar.dma_start(bias_columns[:], bias.rearrange("o (h p) -> p (o h)", p=P))
+        nc.scalar.dma_start(bias_rows[0 : UNITS * CHUNKS, :], bias.rearrange("o (h p) -> (o h) p", p=P))
         for o in range(1, UNITS):
             nc.scalar.dma_start(w_rows[:, o, :], w[o, :].partition_broadcast(P))
 
@@ -45,6 +45,11 @@ def tile_mlp_cutoff_kernel(tc, x, w, bias, offs, out):
 
         identity = held.tile([P, P], F32, name="identity")
         make_identity(nc, identity[:])
+
+        bias_t = psum.tile([P, NETS], F32, name="bias_t", tag="hidden_psum")
+        nc.tensor.transpose(bias_t[:, 0:P], bias_rows[:], identity[:])
+        bias_columns = held.tile([P, UNITS * CHUNKS], F32, name="bias_columns")
+        nc.scalar.copy(bias_columns[:], bias_t[:, 0 : UNITS * CHUNKS])
 
         def look_up(o, b):
             products = work.tile([P, ENTRIES], F32, name="products")

@@ -37,11 +37,11 @@ def tile_mlp_cutoff_kernel(tc, x, w, bias, offs, out):
         for b in range(1, BLOCKS):
             nc.sync.dma_start(x_blocks[b][:], x[b * P : (b + 1) * P, :])
         nc.scalar.dma_start(bias_rows[0 : UNITS * CHUNKS, :], bias.rearrange("o (h p) -> (o h) p", p=P))
-        for o in range(1, UNITS):
-            nc.scalar.dma_start(w_rows[:, o, :], w[o, :].partition_broadcast(P))
-
+        nc.scalar.dma_start(w_rows[:, 1, :], w[1, :].partition_broadcast(P))
+        for o in range(2, UNITS):
+            nc.sync.dma_start(w_rows[:, o, :], w[o, :].partition_broadcast(P))
         last_bias_row = held.tile([P, NETS], F32, name="last_bias_row")
-        nc.scalar.dma_start(last_bias_row[:], bias[UNITS - 1, :].partition_broadcast(P))
+        nc.sync.dma_start(last_bias_row[:], bias[UNITS - 1, :].partition_broadcast(P))
 
         identity = held.tile([P, P], F32, name="identity")
         make_identity(nc, identity[:])

@@ -15,6 +15,7 @@ NETS = 256
 UNITS = 4
 BLOCKS = SAMPLES // P
 CHUNKS = NETS // P
+ALL_CHUNKS = (0, 1)
 
 
 def tile_mlp_cutoff_kernel(tc, x, w, bias, offs, out):
@@ -56,53 +57,69 @@ def tile_mlp_cutoff_kernel(tc, x, w, bias, offs, out):
             nc.vector.tensor_tensor(products[:], x_blocks[b][:].indirect(offsets[:]), w_rows[:, o, :], MULT)
             return products
 
-        def sum_transposed(products):
+        def sum_transposed(products, chunks):
             total_t = psum.tile([P, CHUNKS, P], F32, name="total_t")
-            for h in range(CHUNKS):
+            for h in chunks:
                 first = products[:, h * P : (h + 1) * P]
                 second = products[:, NETS + h * P : NETS + (h + 1) * P]
                 nc.tensor.matmul(total_t[:, h, :], first, identity[:], is_transpose=True, start=True, stop=False)
                 nc.tensor.matmul(total_t[:, h, :], second, identity[:], is_transpose=True, start=False, stop=True)
             return total_t
 
-        def bias_and_relu(o, total_t):
+        def bias_and_relu(o, chunks, total_t):
             hidden_t = work.tile([P, CHUNKS, P], F32, name="hidden_t")
-            for h in range(CHUNKS):
+            for h in chunks:
                 column = o * CHUNKS + h
                 nc.scalar.activation(hidden_t[:, h, :], total_t[:, h, :], RELU, bias=bias_columns[:, column : column + 1])
             return hidden_t
 
-        def back(hidden_t):
+        def back(chunks, hidden_t):
             hidden_psum = psum.tile([P, NETS], F32, name="hidden_psum")
-            for h in range(CHUNKS):
+            for h in chunks:
                 nc.tensor.transpose(hidden_psum[:, h * P : (h + 1) * P], hidden_t[:, h, :], identity[:])
             return hidden_psum
 
-        def copy_out(hidden_psum):
-            hidden = work.tile([P, NETS], F32, name="hidden")
-            nc.scalar.copy(hidden[:], hidden_psum[:])
-            return hidden
+        def copy_out(chunks, hidden_psum, hidden):
+            nets = slice(chunks[0] * P, (chunks[-1] + 1) * P)
+            nc.scalar.copy(hidden[:, nets], hidden_psum[:, nets])
 
-        def sum_bias_relu_on_vector(products):
-            hidden = work.tile([P, NETS], F32, name="hidden")
-            nc.vector.tensor_tensor(hidden[:], products[:, 0:NETS], products[:, NETS:ENTRIES], ADD)
-            nc.vector.tensor_tensor(hidden[:], hidden[:], last_bias_row[:], ADD)
-            nc.vector.tensor_scalar_max(hidden[:], hidden[:], 0.0)
-            return hidden
+        def sum_bias_relu_on_vector(products, hidden):
+            halves = [slice(h * P, (h + 1) * P) for h in range(CHUNKS)]
+            for nets in halves:
+                second = products[:, NETS + nets.start : NETS + nets.stop]
+                nc.vector.tensor_tensor(hidden[:, nets], products[:, nets], second, ADD)
+            for nets in halves:
+                nc.vector.tensor_tensor(hidden[:, nets], hidden[:, nets], last_bias_row[:, nets], ADD)
+            for nets in halves:
+                nc.vector.tensor_scalar_max(hidden[:, nets], hidden[:, nets], 0.0)
 
         def store(o, b, hidden):
             nc.sync.dma_start(out[b * P : (b + 1) * P, o * NETS : (o + 1) * NETS], hidden[:])
 
         earlier = None
-        for o, b in pairs[:-1]:
-            total_t = sum_transposed(look_up(o, b))
+        for o, b in pairs[:-2]:
+            total_t = sum_transposed(look_up(o, b), ALL_CHUNKS)
             if earlier is not None:
-                hidden_psum = back(earlier[2])
-            hidden_t = bias_and_relu(o, total_t)
+                hidden_psum = back(ALL_CHUNKS, earlier[2])
+            hidden_t = bias_and_relu(o, ALL_CHUNKS, total_t)
             if earlier is not None:
-                store(earlier[0], earlier[1], copy_out(hidden_psum))
+                hidden = work.tile([P, NETS], F32, name="hidden")
+                copy_out(ALL_CHUNKS, hidden_psum, hidden)
+                store(earlier[0], earlier[1], hidden)
             earlier = (o, b, hidden_t)
-        o, b = pairs[-1]
-        products = look_up(o, b)
-        store(earlier[0], earlier[1], copy_out(back(earlier[2])))
-        store(o, b, sum_bias_relu_on_vector(products))
+
+        last_two = held.tile([P, 2, NETS], F32, name="last_two")
+        products = look_up(*pairs[-2])
+        totals = [sum_transposed(products, (h,)) for h in ALL_CHUNKS]
+        hidden_psum = back(ALL_CHUNKS, earlier[2])
+        hidden_ts = [bias_and_relu(pairs[-2][0], (h,), totals[h]) for h in ALL_CHUNKS]
+        hidden = work.tile([P, NETS], F32, name="hidden")
+        copy_out(ALL_CHUNKS, hidden_psum, hidden)
+        store(earlier[0], earlier[1], hidden)
+        products = look_up(*pairs[-1])
+        for h in ALL_CHUNKS:
+            copy_out((h,), back((h,), hidden_ts[h]), last_two[:, 0, :])
+        sum_bias_relu_on_vector(products, last_two[:, 1, :])
+        last_outputs = out[(BLOCKS - 2) * P :, (UNITS - 1) * NETS :].rearrange("(b p) n -> p b n", p=P)
+        for h in ALL_CHUNKS:
+            nc.sync.dma_start(last_outputs[:, :, h * P : (h + 1) * P], last_two[:, :, h * P : (h + 1) * P])

@@ -28,19 +28,19 @@ def tile_mlp_cutoff_kernel(tc, x, w, bias, offs, out):
         offsets = held.tile([P, ENTRIES // 16], U16, name="offsets")
         nc.sync.dma_start(offsets[:], offs)
 
-        pairs = sorted(((o, b) for o in range(UNITS) for b in range(BLOCKS)), key=max)
+        pairs = [(o, b) for o in range(UNITS) for b in range(BLOCKS)]
         x_blocks = [held.tile([P, FEATURES], F32, name=f"x_block{b}") for b in range(BLOCKS)]
         w_rows = held.tile([P, UNITS, ENTRIES], F32, name="w_rows")
         bias_rows = held.tile([P, P], F32, name="bias_rows")
         nc.vector.memset(bias_rows[:], 0.0)
         nc.sync.dma_start(x_blocks[0][:], x[0:P, :])
         nc.scalar.dma_start(w_rows[:, 0, :], w[0, :].partition_broadcast(P))
+        w_as_stored = held.tile([P, ENTRIES], F32, name="w_as_stored")
+        nc.gpsimd.memset(w_as_stored[:], 0.0)
+        nc.sync.dma_start(w_as_stored[0:UNITS, :], w)
+        nc.scalar.dma_start(bias_rows[0 : UNITS * CHUNKS, :], bias.rearrange("o (h p) -> (o h) p", p=P))
         for b in range(1, BLOCKS):
             nc.sync.dma_start(x_blocks[b][:], x[b * P : (b + 1) * P, :])
-        nc.scalar.dma_start(bias_rows[0 : UNITS * CHUNKS, :], bias.rearrange("o (h p) -> (o h) p", p=P))
-        nc.scalar.dma_start(w_rows[:, 1, :], w[1, :].partition_broadcast(P))
-        for o in range(2, UNITS):
-            nc.sync.dma_start(w_rows[:, o, :], w[o, :].partition_broadcast(P))
         last_bias_row = held.tile([P, NETS], F32, name="last_bias_row")
         nc.sync.dma_start(last_bias_row[:], bias[UNITS - 1, :].partition_broadcast(P))
 
@@ -51,6 +51,11 @@ def tile_mlp_cutoff_kernel(tc, x, w, bias, offs, out):
         nc.tensor.transpose(bias_t[:, 0:P], bias_rows[:], identity[:])
         bias_columns = held.tile([P, UNITS * CHUNKS], F32, name="bias_columns")
         nc.scalar.copy(bias_columns[:], bias_t[:, 0 : UNITS * CHUNKS])
+
+        def spread_row(o):
+            row_psum = psum.tile([P, ENTRIES], F32, name="row_psum", tag="hidden_psum")
+            nc.tensor.matmul(row_psum[:], identity[:, o : o + 1].to_broadcast([P, P]), w_as_stored[:], start=True, stop=True)
+            nc.scalar.copy(w_rows[:, o, :], row_psum[:])
 
         def look_up(o, b):
             products = work.tile([P, ENTRIES], F32, name="products")
@@ -98,6 +103,8 @@ def tile_mlp_cutoff_kernel(tc, x, w, bias, offs, out):
 
         earlier = None
         for o, b in pairs[:-2]:
+            if b == 0 and o + 1 < UNITS:
+                spread_row(o + 1)
             total_t = sum_transposed(look_up(o, b), ALL_CHUNKS)
             if earlier is not None:
                 hidden_psum = back(ALL_CHUNKS, earlier[2])

@@ -16,6 +16,7 @@ UNITS = 4
 BLOCKS = SAMPLES // P
 CHUNKS = NETS // P
 ALL_CHUNKS = (0, 1)
+HALF_LISTS = (slice(0, ENTRIES // 2), slice(ENTRIES // 2, ENTRIES))
 
 
 def tile_mlp_cutoff_kernel(tc, x, w, bias, offs, out):
@@ -34,7 +35,8 @@ def tile_mlp_cutoff_kernel(tc, x, w, bias, offs, out):
         bias_rows = held.tile([P, P], F32, name="bias_rows")
         nc.vector.memset(bias_rows[:], 0.0)
         nc.sync.dma_start(x_blocks[0][:], x[0:P, :])
-        nc.scalar.dma_start(w_rows[:, 0, :], w[0, :].partition_broadcast(P))
+        for half in HALF_LISTS:
+            nc.scalar.dma_start(w_rows[:, 0, half], w[0, half].partition_broadcast(P))
         w_as_stored = held.tile([P, ENTRIES], F32, name="w_as_stored")
         nc.gpsimd.memset(w_as_stored[:], 0.0)
         nc.sync.dma_start(w_as_stored[0:UNITS, :], w)
@@ -59,7 +61,9 @@ def tile_mlp_cutoff_kernel(tc, x, w, bias, offs, out):
 
         def look_up(o, b):
             products = work.tile([P, ENTRIES], F32, name="products")
-            nc.vector.tensor_tensor(products[:], x_blocks[b][:].indirect(offsets[:]), w_rows[:, o, :], MULT)
+            for part in HALF_LISTS if (o, b) == pairs[0] else [slice(0, ENTRIES)]:
+                listed = offsets[:, part.start // 16 : part.stop // 16]
+                nc.vector.tensor_tensor(products[:, part], x_blocks[b][:].indirect(listed), w_rows[:, o, part], MULT)
             return products
 
         def sum_transposed(products, chunks):

@@ -16,7 +16,8 @@ UNITS = 4
 BLOCKS = SAMPLES // P
 CHUNKS = NETS // P
 ALL_CHUNKS = (0, 1)
-HALF_LISTS = (slice(0, ENTRIES // 2), slice(ENTRIES // 2, ENTRIES))
+FIRST_ENTRIES, SECOND_ENTRIES = slice(0, NETS), slice(NETS, ENTRIES)
+WHOLE_LIST = (slice(0, ENTRIES),)
 
 
 def tile_mlp_cutoff_kernel(tc, x, w, bias, offs, out):
@@ -32,14 +33,14 @@ def tile_mlp_cutoff_kernel(tc, x, w, bias, offs, out):
         pairs = [(o, b) for o in range(UNITS) for b in range(BLOCKS)]
         x_blocks = [held.tile([P, FEATURES], F32, name=f"x_block{b}") for b in range(BLOCKS)]
         w_rows = held.tile([P, UNITS, ENTRIES], F32, name="w_rows")
+        nc.sync.dma_start(x_blocks[0][:], x[0:P, :])
+        for half in (FIRST_ENTRIES, SECOND_ENTRIES):
+            nc.scalar.dma_start(w_rows[:, 0, half], w[0, half].partition_broadcast(P))
+        w_halves = held.tile([P, NETS], F32, name="w_halves")
+        nc.vector.memset(w_halves[:], 0.0)
+        nc.scalar.dma_start(w_halves[0 : 2 * UNITS, :], w.rearrange("o (k n) -> (o k) n", n=NETS))
         bias_rows = held.tile([P, P], F32, name="bias_rows")
         nc.vector.memset(bias_rows[:], 0.0)
-        nc.sync.dma_start(x_blocks[0][:], x[0:P, :])
-        for half in HALF_LISTS:
-            nc.scalar.dma_start(w_rows[:, 0, half], w[0, half].partition_broadcast(P))
-        w_as_stored = held.tile([P, ENTRIES], F32, name="w_as_stored")
-        nc.gpsimd.memset(w_as_stored[:], 0.0)
-        nc.sync.dma_start(w_as_stored[0:UNITS, :], w)
         nc.scalar.dma_start(bias_rows[0 : UNITS * CHUNKS, :], bias.rearrange("o (h p) -> (o h) p", p=P))
         for b in range(1, BLOCKS):
             nc.sync.dma_start(x_blocks[b][:], x[b * P : (b + 1) * P, :])
@@ -49,19 +50,23 @@ def tile_mlp_cutoff_kernel(tc, x, w, bias, offs, out):
         identity = held.tile([P, P], F32, name="identity")
         make_identity(nc, identity[:])
 
+        def spread_row(o):
+            for k, half in enumerate((FIRST_ENTRIES, SECOND_ENTRIES)):
+                half_psum = psum.tile([P, NETS], F32, name="half_psum", tag="hidden_psum")
+                pick = identity[:, 2 * o + k : 2 * o + k + 1].to_broadcast([P, P])
+                nc.tensor.matmul(half_psum[:], pick, w_halves[:], start=True, stop=True)
+                nc.scalar.copy(w_rows[:, o, half], half_psum[:])
+
+        spread_row(1)
+
         bias_t = psum.tile([P, NETS], F32, name="bias_t", tag="hidden_psum")
         nc.tensor.transpose(bias_t[:, 0:P], bias_rows[:], identity[:])
         bias_columns = held.tile([P, UNITS * CHUNKS], F32, name="bias_columns")
         nc.scalar.copy(bias_columns[:], bias_t[:, 0 : UNITS * CHUNKS])
 
-        def spread_row(o):
-            row_psum = psum.tile([P, ENTRIES], F32, name="row_psum", tag="hidden_psum")
-            nc.tensor.matmul(row_psum[:], identity[:, o : o + 1].to_broadcast([P, P]), w_as_stored[:], start=True, stop=True)
-            nc.scalar.copy(w_rows[:, o, :], row_psum[:])
-
-        def look_up(o, b):
+        def look_up(o, b, parts):
             products = work.tile([P, ENTRIES], F32, name="products")
-            for part in HALF_LISTS if (o, b) == pairs[0] else [slice(0, ENTRIES)]:
+            for part in parts:
                 listed = offsets[:, part.start // 16 : part.stop // 16]
                 nc.vector.tensor_tensor(products[:, part], x_blocks[b][:].indirect(listed), w_rows[:, o, part], MULT)
             return products
@@ -96,9 +101,9 @@ def tile_mlp_cutoff_kernel(tc, x, w, bias, offs, out):
             halves = [slice(h * P, (h + 1) * P) for h in range(CHUNKS)]
             for nets in halves:
                 second = products[:, NETS + nets.start : NETS + nets.stop]
-                nc.vector.tensor_tensor(hidden[:, nets], products[:, nets], second, ADD)
+                nc.vector.tensor_tensor(hidden[:, nets], second, last_bias_row[:, nets], ADD)
             for nets in halves:
-                nc.vector.tensor_tensor(hidden[:, nets], hidden[:, nets], last_bias_row[:, nets], ADD)
+                nc.vector.tensor_tensor(hidden[:, nets], hidden[:, nets], products[:, nets], ADD)
             for nets in halves:
                 nc.vector.tensor_scalar_max(hidden[:, nets], hidden[:, nets], 0.0)
 
@@ -107,9 +112,10 @@ def tile_mlp_cutoff_kernel(tc, x, w, bias, offs, out):
 
         earlier = None
         for o, b in pairs[:-2]:
-            if b == 0 and o + 1 < UNITS:
+            if b == 0 and 1 <= o < UNITS - 1:
                 spread_row(o + 1)
-            total_t = sum_transposed(look_up(o, b), ALL_CHUNKS)
+            parts = (FIRST_ENTRIES, SECOND_ENTRIES) if (o, b) == pairs[0] else WHOLE_LIST
+            total_t = sum_transposed(look_up(o, b, parts), ALL_CHUNKS)
             if earlier is not None:
                 hidden_psum = back(ALL_CHUNKS, earlier[2])
             hidden_t = bias_and_relu(o, ALL_CHUNKS, total_t)
@@ -120,14 +126,14 @@ def tile_mlp_cutoff_kernel(tc, x, w, bias, offs, out):
             earlier = (o, b, hidden_t)
 
         last_two = held.tile([P, 2, NETS], F32, name="last_two")
-        products = look_up(*pairs[-2])
+        products = look_up(*pairs[-2], WHOLE_LIST)
         totals = [sum_transposed(products, (h,)) for h in ALL_CHUNKS]
         hidden_psum = back(ALL_CHUNKS, earlier[2])
         hidden_ts = [bias_and_relu(pairs[-2][0], (h,), totals[h]) for h in ALL_CHUNKS]
         hidden = work.tile([P, NETS], F32, name="hidden")
         copy_out(ALL_CHUNKS, hidden_psum, hidden)
         store(earlier[0], earlier[1], hidden)
-        products = look_up(*pairs[-1])
+        products = look_up(*pairs[-1], (SECOND_ENTRIES, FIRST_ENTRIES))
         for h in ALL_CHUNKS:
             copy_out((h,), back((h,), hidden_ts[h]), last_two[:, 0, :])
         sum_bias_relu_on_vector(products, last_two[:, 1, :])

@@ -34,8 +34,7 @@ def tile_mlp_cutoff_kernel(tc, x, w, bias, offs, out):
         x_blocks = [held.tile([P, FEATURES], F32, name=f"x_block{b}") for b in range(BLOCKS)]
         w_rows = held.tile([P, UNITS, ENTRIES], F32, name="w_rows")
         nc.sync.dma_start(x_blocks[0][:], x[0:P, :])
-        for half in (FIRST_ENTRIES, SECOND_ENTRIES):
-            nc.scalar.dma_start(w_rows[:, 0, half], w[0, half].partition_broadcast(P))
+        nc.scalar.dma_start(w_rows[:, 0, :], w[0, :].partition_broadcast(P))
         w_halves = held.tile([P, NETS], F32, name="w_halves")
         nc.vector.memset(w_halves[:], 0.0)
         nc.scalar.dma_start(w_halves[0 : 2 * UNITS, :], w.rearrange("o (k n) -> (o k) n", n=NETS))
@@ -114,8 +113,7 @@ def tile_mlp_cutoff_kernel(tc, x, w, bias, offs, out):
         for o, b in pairs[:-2]:
             if b == 0 and 1 <= o < UNITS - 1:
                 spread_row(o + 1)
-            parts = (FIRST_ENTRIES, SECOND_ENTRIES) if (o, b) == pairs[0] else WHOLE_LIST
-            total_t = sum_transposed(look_up(o, b, parts), ALL_CHUNKS)
+            total_t = sum_transposed(look_up(o, b, WHOLE_LIST), ALL_CHUNKS)
             if earlier is not None:
                 hidden_psum = back(ALL_CHUNKS, earlier[2])
             hidden_t = bias_and_relu(o, ALL_CHUNKS, total_t)

@@ -136,5 +136,4 @@ def tile_mlp_cutoff_kernel(tc, x, w, bias, offs, out):
             copy_out((h,), back((h,), hidden_ts[h]), last_two[:, 0, :])
         sum_bias_relu_on_vector(products, last_two[:, 1, :])
         last_outputs = out[(BLOCKS - 2) * P :, (UNITS - 1) * NETS :].rearrange("(b p) n -> p b n", p=P)
-        for h in ALL_CHUNKS:
-            nc.sync.dma_start(last_outputs[:, :, h * P : (h + 1) * P], last_two[:, :, h * P : (h + 1) * P])
+        nc.sync.dma_start(last_outputs, last_two[:])

import concourse.mybir as mybir
from concourse.masks import make_identity

F32 = mybir.dt.float32
U16 = mybir.dt.uint16
MULT = mybir.AluOpType.mult
ADD = mybir.AluOpType.add
RELU = mybir.ActivationFunctionType.Relu

P = 128
SAMPLES = 512
FEATURES = 512
ENTRIES = 512
NETS = 256
UNITS = 4
BLOCKS = SAMPLES // P
CHUNKS = NETS // P
ALL_CHUNKS = (0, 1)
FIRST_ENTRIES, SECOND_ENTRIES = slice(0, NETS), slice(NETS, ENTRIES)
WHOLE_LIST = (slice(0, ENTRIES),)


def tile_mlp_cutoff_kernel(tc, x, w, bias, offs, out):
    nc = tc.nc
    with (
        tc.tile_pool(name="held", bufs=1) as held,
        tc.tile_pool(name="work", bufs=4) as work,
        tc.psum_pool(name="psum", bufs=4) as psum,
    ):
        offsets = held.tile([P, ENTRIES // 16], U16, name="offsets")
        nc.sync.dma_start(offsets[:], offs)

        pairs = [(o, b) for o in range(UNITS) for b in range(BLOCKS)]
        x_blocks = [held.tile([P, FEATURES], F32, name=f"x_block{b}") for b in range(BLOCKS)]
        w_rows = held.tile([P, UNITS, ENTRIES], F32, name="w_rows")
        nc.sync.dma_start(x_blocks[0][:], x[0:P, :])
        nc.scalar.dma_start(w_rows[:, 0, :], w[0, :].partition_broadcast(P))
        w_halves = held.tile([P, NETS], F32, name="w_halves")
        nc.vector.memset(w_halves[:], 0.0)
        nc.scalar.dma_start(w_halves[0 : 2 * UNITS, :], w.rearrange("o (k n) -> (o k) n", n=NETS))
        bias_rows = held.tile([P, P], F32, name="bias_rows")
        nc.vector.memset(bias_rows[:], 0.0)
        nc.scalar.dma_start(bias_rows[0 : UNITS * CHUNKS, :], bias.rearrange("o (h p) -> (o h) p", p=P))
        for b in range(1, BLOCKS):
            nc.sync.dma_start(x_blocks[b][:], x[b * P : (b + 1) * P, :])
        last_bias_row = held.tile([P, NETS], F32, name="last_bias_row")
        nc.sync.dma_start(last_bias_row[:], bias[UNITS - 1, :].partition_broadcast(P))

        identity = held.tile([P, P], F32, name="identity")
        make_identity(nc, identity[:])

        def spread_row(o):
            for k, half in enumerate((FIRST_ENTRIES, SECOND_ENTRIES)):
                half_psum = psum.tile([P, NETS], F32, name="half_psum", tag="hidden_psum")
                pick = identity[:, 2 * o + k : 2 * o + k + 1].to_broadcast([P, P])
                nc.tensor.matmul(half_psum[:], pick, w_halves[:], start=True, stop=True)
                nc.scalar.copy(w_rows[:, o, half], half_psum[:])

        spread_row(1)

        bias_t = psum.tile([P, NETS], F32, name="bias_t", tag="hidden_psum")
        nc.tensor.transpose(bias_t[:, 0:P], bias_rows[:], identity[:])
        bias_columns = held.tile([P, UNITS * CHUNKS], F32, name="bias_columns")
        nc.scalar.copy(bias_columns[:], bias_t[:, 0 : UNITS * CHUNKS])

        def look_up(o, b, parts):
            products = work.tile([P, ENTRIES], F32, name="products")
            for part in parts:
                listed = offsets[:, part.start // 16 : part.stop // 16]
                nc.vector.tensor_tensor(products[:, part], x_blocks[b][:].indirect(listed), w_rows[:, o, part], MULT)
            return products

        def sum_transposed(products, chunks):
            total_t = psum.tile([P, CHUNKS, P], F32, name="total_t")
            for h in chunks:
                first = products[:, h * P : (h + 1) * P]
                second = products[:, NETS + h * P : NETS + (h + 1) * P]
                nc.tensor.matmul(total_t[:, h, :], first, identity[:], is_transpose=True, start=True, stop=False)
                nc.tensor.matmul(total_t[:, h, :], second, identity[:], is_transpose=True, start=False, stop=True)
            return total_t

        def bias_and_relu(o, chunks, total_t):
            hidden_t = work.tile([P, CHUNKS, P], F32, name="hidden_t")
            for h in chunks:
                column = o * CHUNKS + h
                nc.scalar.activation(hidden_t[:, h, :], total_t[:, h, :], RELU, bias=bias_columns[:, column : column + 1])
            return hidden_t

        def back(chunks, hidden_t):
            hidden_psum = psum.tile([P, NETS], F32, name="hidden_psum")
            for h in chunks:
                nc.tensor.transpose(hidden_psum[:, h * P : (h + 1) * P], hidden_t[:, h, :], identity[:])
            return hidden_psum

        def copy_out(chunks, hidden_psum, hidden):
            nets = slice(chunks[0] * P, (chunks[-1] + 1) * P)
            nc.scalar.copy(hidden[:, nets], hidden_psum[:, nets])

        def sum_bias_relu_on_vector(products, hidden):
            halves = [slice(h * P, (h + 1) * P) for h in range(CHUNKS)]
            for nets in halves:
                second = products[:, NETS + nets.start : NETS + nets.stop]
                nc.vector.tensor_tensor(hidden[:, nets], second, last_bias_row[:, nets], ADD)
            for nets in halves:
                nc.vector.tensor_tensor(hidden[:, nets], hidden[:, nets], products[:, nets], ADD)
            for nets in halves:
                nc.vector.tensor_scalar_max(hidden[:, nets], hidden[:, nets], 0.0)

        def store(o, b, hidden):
            nc.sync.dma_start(out[b * P : (b + 1) * P, o * NETS : (o + 1) * NETS], hidden[:])

        earlier = None
        for o, b in pairs[:-2]:
            if b == 0 and 1 <= o < UNITS - 1:
                spread_row(o + 1)
            total_t = sum_transposed(look_up(o, b, WHOLE_LIST), ALL_CHUNKS)
            if earlier is not None:
                hidden_psum = back(ALL_CHUNKS, earlier[2])
            hidden_t = bias_and_relu(o, ALL_CHUNKS, total_t)
            if earlier is not None:
                hidden = work.tile([P, NETS], F32, name="hidden")
                copy_out(ALL_CHUNKS, hidden_psum, hidden)
                store(earlier[0], earlier[1], hidden)
            earlier = (o, b, hidden_t)

        last_two = held.tile([P, 2, NETS], F32, name="last_two")
        products = look_up(*pairs[-2], WHOLE_LIST)
        totals = [sum_transposed(products, (h,)) for h in ALL_CHUNKS]
        hidden_psum = back(ALL_CHUNKS, earlier[2])
        hidden_ts = [bias_and_relu(pairs[-2][0], (h,), totals[h]) for h in ALL_CHUNKS]
        hidden = work.tile([P, NETS], F32, name="hidden")
        copy_out(ALL_CHUNKS, hidden_psum, hidden)
        store(earlier[0], earlier[1], hidden)
        products = look_up(*pairs[-1], (SECOND_ENTRIES, FIRST_ENTRIES))
        for h in ALL_CHUNKS:
            copy_out((h,), back((h,), hidden_ts[h]), last_two[:, 0, :])
        sum_bias_relu_on_vector(products, last_two[:, 1, :])
        last_outputs = out[(BLOCKS - 2) * P :, (UNITS - 1) * NETS :].rearrange("(b p) n -> p b n", p=P)
        nc.sync.dma_start(last_outputs, last_two[:])
